import numpy as np
import ml_dtypes

BF16 = ml_dtypes.bfloat16


def bf(x):
    return np.asarray(x, np.float32).astype(BF16)


def f32(x):
    return np.asarray(x, np.float32)


def f64(x):
    return np.asarray(x).astype(np.float64)


def striped(idx):
    return np.tile(idx.reshape(-1, 16).T, (8, 1))


S, D, M, NBF, E, N = 2048, 128, 256, 512, 256, 512


def silu(v):
    return v / (1.0 + np.exp(-v))


def setup_inputs():
    return {"table": bf(np.random.standard_normal((S, D))), "w_src": bf(np.random.standard_normal((D, M)) / np.sqrt(D + D)), "w_dst": bf(np.random.standard_normal((D, M)) / np.sqrt(D + D)), "b_proj": f32(0.1 * np.random.standard_normal((M, 1))), "x_edge": bf(np.random.standard_normal((NBF, E))), "w_dist": bf(np.random.standard_normal((NBF, M)) / np.sqrt(NBF)), "b_dist": f32(0.1 * np.random.standard_normal((M, 1))), "offs": striped(np.random.permutation(np.tile(np.arange(S), 2))[:N])}


def reference(table, w_src, w_dst, b_proj, x_edge, w_dist, b_dist, offs):
    idx = offs[:16].T.reshape(-1)
    t = f64(table)
    p = f64(w_src).T @ t[idx[:E]].T + f64(w_dst).T @ t[idx[E:]].T + f64(b_proj)
    q = f64(w_dist).T @ f64(x_edge) + f64(b_dist)
    return silu(p) * silu(q)

@@ -1,0 +1,93 @@
+import concourse.mybir as mybir
+from concourse.masks import make_identity
+
+BF16, F32, U16 = mybir.dt.bfloat16, mybir.dt.float32, mybir.dt.uint16
+SILU = mybir.ActivationFunctionType.Silu
+
+P = 128
+NODES = 2048
+EDGES = 256
+FEATURES = 256
+HALVES = FEATURES // P
+RADIAL = 512
+CHUNKS = RADIAL // P
+LIST_COLUMNS = EDGES // 16
+GROUP = 512
+BLOCKS = GROUP // P
+GROUPS = NODES // GROUP
+
+FLOPS = 2 * FEATURES * EDGES * (P + P + RADIAL)
+
+
+def tile_messageblock_kernel(tc, table, w_src, w_dst, b_proj, x_edge, w_dist, b_dist, offs, out):
+    nc = tc.nc
+    with (
+        tc.tile_pool(name="held", bufs=1) as held,
+        tc.psum_pool(name="psum", bufs=1) as psum,
+    ):
+        offsets = held.tile([P, 2 * LIST_COLUMNS], U16, name="offsets")
+        nc.sync.dma_start(offsets[:], offs)
+
+        identity = held.tile([P, P], BF16, name="identity")
+        make_identity(nc, identity[:])
+
+        rows = []
+        for g in range(GROUPS):
+            group_rows = held.tile([P, BLOCKS, P], BF16, name=f"rows{g}")
+            queue = nc.sync if g % 2 == 0 else nc.scalar
+            queue.dma_start(
+                group_rows[:], table[g * GROUP : (g + 1) * GROUP, :].rearrange("(b p) k -> p b k", p=P)
+            )
+            rows.append(group_rows)
+
+        edge_x = held.tile([P, CHUNKS, EDGES], BF16, name="edge_x")
+        nc.sync.dma_start(edge_x[:], x_edge.rearrange("(p c) e -> p c e", c=CHUNKS))
+        dist_w = held.tile([P, CHUNKS, FEATURES], BF16, name="dist_w")
+        nc.scalar.dma_start(dist_w[:], w_dist.rearrange("(p c) m -> p c m", c=CHUNKS))
+
+        src_w = held.tile([P, FEATURES], BF16, name="src_w")
+        nc.sync.dma_start(src_w[:], w_src)
+        dst_w = held.tile([P, FEATURES], BF16, name="dst_w")
+        nc.scalar.dma_start(dst_w[:], w_dst)
+
+        dist_b = held.tile([P, HALVES], F32, name="dist_b")
+        proj_b = held.tile([P, HALVES], F32, name="proj_b")
+        with nc.allow_non_contiguous_dma(reason="one float32 of a bias to each partition"):
+            nc.sync.dma_start(dist_b[:], b_dist.rearrange("(h p) o -> p (h o)", p=P))
+            nc.scalar.dma_start(proj_b[:], b_proj.rearrange("(h p) o -> p (h o)", p=P))
+
+        table_t = held.tile([P, NODES], BF16, name="table_t")
+        for g in range(GROUPS):
+            flipped = psum.tile([P, GROUP], BF16, name=f"flipped{g}")
+            for b in range(BLOCKS):
+                nc.tensor.transpose(flipped[:, b * P : (b + 1) * P], rows[g][:, b, :], identity[:])
+            if g % 2 == 0:
+                nc.vector.tensor_copy(table_t[:, g * GROUP : (g + 1) * GROUP], flipped[:])
+            else:
+                nc.scalar.copy(table_t[:, g * GROUP : (g + 1) * GROUP], flipped[:])
+
+        q_act = []
+        for h in range(HALVES):
+            features = slice(h * P, (h + 1) * P)
+            q_sum = psum.tile([P, EDGES], F32, name=f"q_sum{h}")
+            for c in range(CHUNKS):
+                nc.tensor.matmul(
+                    q_sum[:], dist_w[:, c, features], edge_x[:, c, :], start=(c == 0), stop=(c == CHUNKS - 1)
+                )
+            q_silu = held.tile([P, EDGES], F32, name=f"q_silu{h}")
+            nc.scalar.activation(q_silu[:], q_sum[:], SILU, bias=dist_b[:, h : h + 1])
+            q_act.append(q_silu)
+
+        sources = table_t[:].indirect(offsets[:, 0:LIST_COLUMNS])
+        targets = table_t[:].indirect(offsets[:, LIST_COLUMNS : 2 * LIST_COLUMNS])
+        for h in range(HALVES):
+            features = slice(h * P, (h + 1) * P)
+            p_sum = psum.tile([P, EDGES], F32, name=f"p_sum{h}")
+            nc.tensor.matmul(p_sum[:], src_w[:, features], sources, start=True, stop=False)
+            nc.tensor.matmul(p_sum[:], dst_w[:, features], targets, start=False, stop=True)
+            p_silu = held.tile([P, EDGES], F32, name=f"p_silu{h}")
+            nc.scalar.activation(p_silu[:], p_sum[:], SILU, bias=proj_b[:, h : h + 1])
+            message = held.tile([P, EDGES], F32, name=f"message{h}")
+            nc.vector.tensor_mul(message[:], p_silu[:], q_act[h][:])
+            queue = nc.sync if h % 2 == 0 else nc.scalar
+            queue.dma_start(out[features, :], message[:])

@@ -31,6 +31,11 @@ def tile_messageblock_kernel(tc, table, w_src, w_dst, b_proj, x_edge, w_dist, b_
         identity = held.tile([P, P], BF16, name="identity")
         make_identity(nc, identity[:])
 
+        edge_x = held.tile([P, CHUNKS, EDGES], BF16, name="edge_x")
+        nc.sync.dma_start(edge_x[:], x_edge.rearrange("(p c) e -> p c e", c=CHUNKS))
+        dist_w = held.tile([P, CHUNKS, FEATURES], BF16, name="dist_w")
+        nc.scalar.dma_start(dist_w[:], w_dist.rearrange("(p c) m -> p c m", c=CHUNKS))
+
         rows = []
         for g in range(GROUPS):
             group_rows = held.tile([P, BLOCKS, P], BF16, name=f"rows{g}")
@@ -39,11 +44,6 @@ def tile_messageblock_kernel(tc, table, w_src, w_dst, b_proj, x_edge, w_dist, b_
                 group_rows[:], table[g * GROUP : (g + 1) * GROUP, :].rearrange("(b p) k -> p b k", p=P)
             )
             rows.append(group_rows)
-
-        edge_x = held.tile([P, CHUNKS, EDGES], BF16, name="edge_x")
-        nc.sync.dma_start(edge_x[:], x_edge.rearrange("(p c) e -> p c e", c=CHUNKS))
-        dist_w = held.tile([P, CHUNKS, FEATURES], BF16, name="dist_w")
-        nc.scalar.dma_start(dist_w[:], w_dist.rearrange("(p c) m -> p c m", c=CHUNKS))
 
         src_w = held.tile([P, FEATURES], BF16, name="src_w")
         nc.sync.dma_start(src_w[:], w_src)
@@ -56,16 +56,6 @@ def tile_messageblock_kernel(tc, table, w_src, w_dst, b_proj, x_edge, w_dist, b_
             nc.sync.dma_start(dist_b[:], b_dist.rearrange("(h p) o -> p (h o)", p=P))
             nc.scalar.dma_start(proj_b[:], b_proj.rearrange("(h p) o -> p (h o)", p=P))
 
-        table_t = held.tile([P, NODES], BF16, name="table_t")
-        for g in range(GROUPS):
-            flipped = psum.tile([P, GROUP], BF16, name=f"flipped{g}")
-            for b in range(BLOCKS):
-                nc.tensor.transpose(flipped[:, b * P : (b + 1) * P], rows[g][:, b, :], identity[:])
-            if g % 2 == 0:
-                nc.vector.tensor_copy(table_t[:, g * GROUP : (g + 1) * GROUP], flipped[:])
-            else:
-                nc.scalar.copy(table_t[:, g * GROUP : (g + 1) * GROUP], flipped[:])
-
         q_act = []
         for h in range(HALVES):
             features = slice(h * P, (h + 1) * P)
@@ -77,6 +67,13 @@ def tile_messageblock_kernel(tc, table, w_src, w_dst, b_proj, x_edge, w_dist, b_
             q_silu = held.tile([P, EDGES], F32, name=f"q_silu{h}")
             nc.scalar.activation(q_silu[:], q_sum[:], SILU, bias=dist_b[:, h : h + 1])
             q_act.append(q_silu)
+
+        table_t = held.tile([P, NODES], BF16, name="table_t")
+        for g in range(GROUPS):
+            flipped = psum.tile([P, GROUP], BF16, name=f"flipped{g}")
+            for b in range(BLOCKS):
+                nc.tensor.transpose(flipped[:, b * P : (b + 1) * P], rows[g][:, b, :], identity[:])
+            nc.vector.tensor_copy(table_t[:, g * GROUP : (g + 1) * GROUP], flipped[:])
 
         sources = table_t[:].indirect(offsets[:, 0:LIST_COLUMNS])
         targets = table_t[:].indirect(offsets[:, LIST_COLUMNS : 2 * LIST_COLUMNS])

@@ -15,6 +15,8 @@ LIST_COLUMNS = EDGES // 16
 GROUP = 512
 BLOCKS = GROUP // P
 GROUPS = NODES // GROUP
+WARM_COLUMNS = 512
+WARM_MATMULS = 4
 
 FLOPS = 2 * FEATURES * EDGES * (P + P + RADIAL)
 
@@ -24,12 +26,22 @@ def tile_messageblock_kernel(tc, table, w_src, w_dst, b_proj, x_edge, w_dist, b_
     with (
         tc.tile_pool(name="held", bufs=1) as held,
         tc.psum_pool(name="psum", bufs=1) as psum,
+        tc.psum_pool(name="flip", bufs=3) as flip,
     ):
         offsets = held.tile([P, 2 * LIST_COLUMNS], U16, name="offsets")
         nc.sync.dma_start(offsets[:], offs)
 
         identity = held.tile([P, P], BF16, name="identity")
         make_identity(nc, identity[:])
+
+        zeros = held.tile([P, WARM_COLUMNS], BF16, name="zeros")
+        nc.vector.memset(zeros[:], 0.0)
+        warm = psum.tile([P, WARM_COLUMNS], F32, name="warm")
+        for i in range(WARM_MATMULS):
+            nc.tensor.matmul(warm[:], zeros[:, 0:P], zeros[:], start=True, stop=True)
+
+        table_load = held.tile([P, 1], F32, name="table_load")
+        nc.scalar.activation(table_load[:], zeros[:, 0:1], SILU)
 
         edge_x = held.tile([P, CHUNKS, EDGES], BF16, name="edge_x")
         nc.sync.dma_start(edge_x[:], x_edge.rearrange("(p c) e -> p c e", c=CHUNKS))
@@ -70,7 +82,7 @@ def tile_messageblock_kernel(tc, table, w_src, w_dst, b_proj, x_edge, w_dist, b_
 
         table_t = held.tile([P, NODES], BF16, name="table_t")
         for g in range(GROUPS):
-            flipped = psum.tile([P, GROUP], BF16, name=f"flipped{g}")
+            flipped = flip.tile([P, GROUP], BF16, name="flipped")
             for b in range(BLOCKS):
                 nc.tensor.transpose(flipped[:, b * P : (b + 1) * P], rows[g][:, b, :], identity[:])
             nc.vector.tensor_copy(table_t[:, g * GROUP : (g + 1) * GROUP], flipped[:])

@@ -26,17 +26,14 @@ def tile_messageblock_kernel(tc, table, w_src, w_dst, b_proj, x_edge, w_dist, b_
     with (
         tc.tile_pool(name="held", bufs=1) as held,
         tc.psum_pool(name="psum", bufs=1) as psum,
-        tc.psum_pool(name="flip", bufs=3) as flip,
+        tc.psum_pool(name="flip", bufs=GROUPS) as flip,
     ):
-        offsets = held.tile([P, 2 * LIST_COLUMNS], U16, name="offsets")
-        nc.sync.dma_start(offsets[:], offs)
-
         identity = held.tile([P, P], BF16, name="identity")
         make_identity(nc, identity[:])
 
         zeros = held.tile([P, WARM_COLUMNS], BF16, name="zeros")
         nc.vector.memset(zeros[:], 0.0)
-        warm = psum.tile([P, WARM_COLUMNS], F32, name="warm")
+        warm = flip.tile([P, WARM_COLUMNS], F32, name="warm", tag="flipped")
         for i in range(WARM_MATMULS):
             nc.tensor.matmul(warm[:], zeros[:, 0:P], zeros[:], start=True, stop=True)
 
@@ -53,10 +50,12 @@ def tile_messageblock_kernel(tc, table, w_src, w_dst, b_proj, x_edge, w_dist, b_
             group_rows = held.tile([P, BLOCKS, P], BF16, name=f"rows{g}")
             queue = nc.sync if g % 2 == 0 else nc.scalar
             queue.dma_start(
-                group_rows[:], table[g * GROUP : (g + 1) * GROUP, :].rearrange("(b p) k -> p b k", p=P)
+                group_rows[:], table[g * GROUP : (g + 1) * GROUP, :].rearrange("(p b) k -> p b k", b=BLOCKS)
             )
             rows.append(group_rows)
 
+        offsets = held.tile([P, 2 * LIST_COLUMNS], U16, name="offsets")
+        nc.sync.dma_start(offsets[:], offs)
         src_w = held.tile([P, FEATURES], BF16, name="src_w")
         nc.sync.dma_start(src_w[:], w_src)
         dst_w = held.tile([P, FEATURES], BF16, name="dst_w")
@@ -82,10 +81,15 @@ def tile_messageblock_kernel(tc, table, w_src, w_dst, b_proj, x_edge, w_dist, b_
 
         table_t = held.tile([P, NODES], BF16, name="table_t")
         for g in range(GROUPS):
-            flipped = flip.tile([P, GROUP], BF16, name="flipped")
+            flipped = flip.tile([P, BLOCKS, P], BF16, name="flipped")
             for b in range(BLOCKS):
-                nc.tensor.transpose(flipped[:, b * P : (b + 1) * P], rows[g][:, b, :], identity[:])
-            nc.vector.tensor_copy(table_t[:, g * GROUP : (g + 1) * GROUP], flipped[:])
+                nc.tensor.transpose(flipped[:, b, :], rows[g][:, b, :], identity[:])
+            in_order = flipped[:].rearrange("k b p -> k p b")
+            columns = table_t[:, g * GROUP : (g + 1) * GROUP].rearrange("k (p b) -> k p b", b=BLOCKS)
+            if g % 2 == 0:
+                nc.vector.tensor_copy(columns, in_order)
+            else:
+                nc.scalar.copy(columns, in_order)
 
         sources = table_t[:].indirect(offsets[:, 0:LIST_COLUMNS])
         targets = table_t[:].indirect(offsets[:, LIST_COLUMNS : 2 * LIST_COLUMNS])

@@ -15,6 +15,8 @@ LIST_COLUMNS = EDGES // 16
 GROUP = 512
 BLOCKS = GROUP // P
 GROUPS = NODES // GROUP
+SQUARE = 32
+QUARTERS = P // SQUARE
 WARM_COLUMNS = 512
 WARM_MATMULS = 4
 
@@ -26,14 +28,17 @@ def tile_messageblock_kernel(tc, table, w_src, w_dst, b_proj, x_edge, w_dist, b_
     with (
         tc.tile_pool(name="held", bufs=1) as held,
         tc.psum_pool(name="psum", bufs=1) as psum,
-        tc.psum_pool(name="flip", bufs=GROUPS) as flip,
+        tc.psum_pool(name="flip", bufs=3) as flip,
     ):
+        offsets = held.tile([P, 2 * LIST_COLUMNS], U16, name="offsets")
+        nc.sync.dma_start(offsets[:], offs)
+
         identity = held.tile([P, P], BF16, name="identity")
         make_identity(nc, identity[:])
 
         zeros = held.tile([P, WARM_COLUMNS], BF16, name="zeros")
         nc.vector.memset(zeros[:], 0.0)
-        warm = flip.tile([P, WARM_COLUMNS], F32, name="warm", tag="flipped")
+        warm = psum.tile([P, WARM_COLUMNS], F32, name="warm")
         for i in range(WARM_MATMULS):
             nc.tensor.matmul(warm[:], zeros[:, 0:P], zeros[:], start=True, stop=True)
 
@@ -45,27 +50,29 @@ def tile_messageblock_kernel(tc, table, w_src, w_dst, b_proj, x_edge, w_dist, b_
         dist_w = held.tile([P, CHUNKS, FEATURES], BF16, name="dist_w")
         nc.scalar.dma_start(dist_w[:], w_dist.rearrange("(p c) m -> p c m", c=CHUNKS))
 
+        bias_runs = held.tile([P, P], F32, name="bias_runs", align_bytes=64)
+        nc.vector.memset(bias_runs[:], 0.0)
+        run_slots = bias_runs[:, 0 : HALVES * SQUARE].rearrange("(r s) (h i) -> s r h i", s=SQUARE, i=SQUARE)
+        nc.sync.dma_start(run_slots[0], b_dist.rearrange("(h r i) o -> r h (i o)", h=HALVES, r=QUARTERS))
+        nc.scalar.dma_start(run_slots[1], b_proj.rearrange("(h r i) o -> r h (i o)", h=HALVES, r=QUARTERS))
+        biases = held.tile([P, P], F32, name="biases", align_bytes=64)
+        nc.vector.transpose(biases[:], bias_runs[:])
+        dist_b = [biases[:, h * SQUARE : h * SQUARE + 1] for h in range(HALVES)]
+        proj_b = [biases[:, h * SQUARE + 1 : h * SQUARE + 2] for h in range(HALVES)]
+
         rows = []
         for g in range(GROUPS):
             group_rows = held.tile([P, BLOCKS, P], BF16, name=f"rows{g}")
             queue = nc.sync if g % 2 == 0 else nc.scalar
             queue.dma_start(
-                group_rows[:], table[g * GROUP : (g + 1) * GROUP, :].rearrange("(p b) k -> p b k", b=BLOCKS)
+                group_rows[:], table[g * GROUP : (g + 1) * GROUP, :].rearrange("(b p) k -> p b k", p=P)
             )
             rows.append(group_rows)
 
-        offsets = held.tile([P, 2 * LIST_COLUMNS], U16, name="offsets")
-        nc.sync.dma_start(offsets[:], offs)
         src_w = held.tile([P, FEATURES], BF16, name="src_w")
         nc.sync.dma_start(src_w[:], w_src)
         dst_w = held.tile([P, FEATURES], BF16, name="dst_w")
         nc.scalar.dma_start(dst_w[:], w_dst)
-
-        dist_b = held.tile([P, HALVES], F32, name="dist_b")
-        proj_b = held.tile([P, HALVES], F32, name="proj_b")
-        with nc.allow_non_contiguous_dma(reason="one float32 of a bias to each partition"):
-            nc.sync.dma_start(dist_b[:], b_dist.rearrange("(h p) o -> p (h o)", p=P))
-            nc.scalar.dma_start(proj_b[:], b_proj.rearrange("(h p) o -> p (h o)", p=P))
 
         q_act = []
         for h in range(HALVES):
@@ -76,20 +83,15 @@ def tile_messageblock_kernel(tc, table, w_src, w_dst, b_proj, x_edge, w_dist, b_
                     q_sum[:], dist_w[:, c, features], edge_x[:, c, :], start=(c == 0), stop=(c == CHUNKS - 1)
                 )
             q_silu = held.tile([P, EDGES], F32, name=f"q_silu{h}")
-            nc.scalar.activation(q_silu[:], q_sum[:], SILU, bias=dist_b[:, h : h + 1])
+            nc.scalar.activation(q_silu[:], q_sum[:], SILU, bias=dist_b[h])
             q_act.append(q_silu)
 
         table_t = held.tile([P, NODES], BF16, name="table_t")
         for g in range(GROUPS):
-            flipped = flip.tile([P, BLOCKS, P], BF16, name="flipped")
+            flipped = flip.tile([P, GROUP], BF16, name="flipped")
             for b in range(BLOCKS):
-                nc.tensor.transpose(flipped[:, b, :], rows[g][:, b, :], identity[:])
-            in_order = flipped[:].rearrange("k b p -> k p b")
-            columns = table_t[:, g * GROUP : (g + 1) * GROUP].rearrange("k (p b) -> k p b", b=BLOCKS)
-            if g % 2 == 0:
-                nc.vector.tensor_copy(columns, in_order)
-            else:
-                nc.scalar.copy(columns, in_order)
+                nc.tensor.transpose(flipped[:, b * P : (b + 1) * P], rows[g][:, b, :], identity[:])
+            nc.vector.tensor_copy(table_t[:, g * GROUP : (g + 1) * GROUP], flipped[:])
 
         sources = table_t[:].indirect(offsets[:, 0:LIST_COLUMNS])
         targets = table_t[:].indirect(offsets[:, LIST_COLUMNS : 2 * LIST_COLUMNS])
@@ -99,7 +101,7 @@ def tile_messageblock_kernel(tc, table, w_src, w_dst, b_proj, x_edge, w_dist, b_
             nc.tensor.matmul(p_sum[:], src_w[:, features], sources, start=True, stop=False)
             nc.tensor.matmul(p_sum[:], dst_w[:, features], targets, start=False, stop=True)
             p_silu = held.tile([P, EDGES], F32, name=f"p_silu{h}")
-            nc.scalar.activation(p_silu[:], p_sum[:], SILU, bias=proj_b[:, h : h + 1])
+            nc.scalar.activation(p_silu[:], p_sum[:], SILU, bias=proj_b[h])
             message = held.tile([P, EDGES], F32, name=f"message{h}")
             nc.vector.tensor_mul(message[:], p_silu[:], q_act[h][:])
             queue = nc.sync if h % 2 == 0 else nc.scalar

@@ -12,7 +12,7 @@ HALVES = FEATURES // P
 RADIAL = 512
 CHUNKS = RADIAL // P
 LIST_COLUMNS = EDGES // 16
-GROUP = 512
+GROUP = 256
 BLOCKS = GROUP // P
 GROUPS = NODES // GROUP
 SQUARE = 32

@@ -12,7 +12,7 @@ HALVES = FEATURES // P
 RADIAL = 512
 CHUNKS = RADIAL // P
 LIST_COLUMNS = EDGES // 16
-GROUP = 256
+GROUP = 512
 BLOCKS = GROUP // P
 GROUPS = NODES // GROUP
 SQUARE = 32
@@ -42,9 +42,6 @@ def tile_messageblock_kernel(tc, table, w_src, w_dst, b_proj, x_edge, w_dist, b_
         for i in range(WARM_MATMULS):
             nc.tensor.matmul(warm[:], zeros[:, 0:P], zeros[:], start=True, stop=True)
 
-        table_load = held.tile([P, 1], F32, name="table_load")
-        nc.scalar.activation(table_load[:], zeros[:, 0:1], SILU)
-
         edge_x = held.tile([P, CHUNKS, EDGES], BF16, name="edge_x")
         nc.sync.dma_start(edge_x[:], x_edge.rearrange("(p c) e -> p c e", c=CHUNKS))
         dist_w = held.tile([P, CHUNKS, FEATURES], BF16, name="dist_w")
@@ -73,6 +70,9 @@ def tile_messageblock_kernel(tc, table, w_src, w_dst, b_proj, x_edge, w_dist, b_
         nc.sync.dma_start(src_w[:], w_src)
         dst_w = held.tile([P, FEATURES], BF16, name="dst_w")
         nc.scalar.dma_start(dst_w[:], w_dst)
+
+        table_load = held.tile([P, 1], F32, name="table_load")
+        nc.scalar.activation(table_load[:], zeros[:, 0:1], SILU)
 
         q_act = []
         for h in range(HALVES):

@@ -42,21 +42,6 @@ def tile_messageblock_kernel(tc, table, w_src, w_dst, b_proj, x_edge, w_dist, b_
         for i in range(WARM_MATMULS):
             nc.tensor.matmul(warm[:], zeros[:, 0:P], zeros[:], start=True, stop=True)
 
-        edge_x = held.tile([P, CHUNKS, EDGES], BF16, name="edge_x")
-        nc.sync.dma_start(edge_x[:], x_edge.rearrange("(p c) e -> p c e", c=CHUNKS))
-        dist_w = held.tile([P, CHUNKS, FEATURES], BF16, name="dist_w")
-        nc.scalar.dma_start(dist_w[:], w_dist.rearrange("(p c) m -> p c m", c=CHUNKS))
-
-        bias_runs = held.tile([P, P], F32, name="bias_runs", align_bytes=64)
-        nc.vector.memset(bias_runs[:], 0.0)
-        run_slots = bias_runs[:, 0 : HALVES * SQUARE].rearrange("(r s) (h i) -> s r h i", s=SQUARE, i=SQUARE)
-        nc.sync.dma_start(run_slots[0], b_dist.rearrange("(h r i) o -> r h (i o)", h=HALVES, r=QUARTERS))
-        nc.scalar.dma_start(run_slots[1], b_proj.rearrange("(h r i) o -> r h (i o)", h=HALVES, r=QUARTERS))
-        biases = held.tile([P, P], F32, name="biases", align_bytes=64)
-        nc.vector.transpose(biases[:], bias_runs[:])
-        dist_b = [biases[:, h * SQUARE : h * SQUARE + 1] for h in range(HALVES)]
-        proj_b = [biases[:, h * SQUARE + 1 : h * SQUARE + 2] for h in range(HALVES)]
-
         rows = []
         for g in range(GROUPS):
             group_rows = held.tile([P, BLOCKS, P], BF16, name=f"rows{g}")
@@ -71,20 +56,23 @@ def tile_messageblock_kernel(tc, table, w_src, w_dst, b_proj, x_edge, w_dist, b_
         dst_w = held.tile([P, FEATURES], BF16, name="dst_w")
         nc.scalar.dma_start(dst_w[:], w_dst)
 
+        bias_runs = held.tile([P, P], F32, name="bias_runs", align_bytes=64)
+        nc.vector.memset(bias_runs[:], 0.0)
+        run_slots = bias_runs[:, 0 : HALVES * SQUARE].rearrange("(r s) (h i) -> s r h i", s=SQUARE, i=SQUARE)
+        nc.sync.dma_start(run_slots[0], b_dist.rearrange("(h r i) o -> r h (i o)", h=HALVES, r=QUARTERS))
+        nc.scalar.dma_start(run_slots[1], b_proj.rearrange("(h r i) o -> r h (i o)", h=HALVES, r=QUARTERS))
+        biases = held.tile([P, P], F32, name="biases", align_bytes=64)
+        nc.vector.transpose(biases[:], bias_runs[:])
+        dist_b = [biases[:, h * SQUARE : h * SQUARE + 1] for h in range(HALVES)]
+        proj_b = [biases[:, h * SQUARE + 1 : h * SQUARE + 2] for h in range(HALVES)]
+
+        edge_x = held.tile([P, CHUNKS, EDGES], BF16, name="edge_x")
+        nc.sync.dma_start(edge_x[:], x_edge.rearrange("(p c) e -> p c e", c=CHUNKS))
+        dist_w = held.tile([P, CHUNKS, FEATURES], BF16, name="dist_w")
+        nc.scalar.dma_start(dist_w[:], w_dist.rearrange("(p c) m -> p c m", c=CHUNKS))
+
         table_load = held.tile([P, 1], F32, name="table_load")
         nc.scalar.activation(table_load[:], zeros[:, 0:1], SILU)
-
-        q_act = []
-        for h in range(HALVES):
-            features = slice(h * P, (h + 1) * P)
-            q_sum = psum.tile([P, EDGES], F32, name=f"q_sum{h}")
-            for c in range(CHUNKS):
-                nc.tensor.matmul(
-                    q_sum[:], dist_w[:, c, features], edge_x[:, c, :], start=(c == 0), stop=(c == CHUNKS - 1)
-                )
-            q_silu = held.tile([P, EDGES], F32, name=f"q_silu{h}")
-            nc.scalar.activation(q_silu[:], q_sum[:], SILU, bias=dist_b[h])
-            q_act.append(q_silu)
 
         table_t = held.tile([P, NODES], BF16, name="table_t")
         for g in range(GROUPS):
@@ -95,6 +83,7 @@ def tile_messageblock_kernel(tc, table, w_src, w_dst, b_proj, x_edge, w_dist, b_
 
         sources = table_t[:].indirect(offsets[:, 0:LIST_COLUMNS])
         targets = table_t[:].indirect(offsets[:, LIST_COLUMNS : 2 * LIST_COLUMNS])
+        p_act = []
         for h in range(HALVES):
             features = slice(h * P, (h + 1) * P)
             p_sum = psum.tile([P, EDGES], F32, name=f"p_sum{h}")
@@ -102,7 +91,18 @@ def tile_messageblock_kernel(tc, table, w_src, w_dst, b_proj, x_edge, w_dist, b_
             nc.tensor.matmul(p_sum[:], dst_w[:, features], targets, start=False, stop=True)
             p_silu = held.tile([P, EDGES], F32, name=f"p_silu{h}")
             nc.scalar.activation(p_silu[:], p_sum[:], SILU, bias=proj_b[h])
+            p_act.append(p_silu)
+
+        for h in range(HALVES):
+            features = slice(h * P, (h + 1) * P)
+            q_sum = psum.tile([P, EDGES], F32, name=f"q_sum{h}")
+            for c in range(CHUNKS):
+                nc.tensor.matmul(
+                    q_sum[:], dist_w[:, c, features], edge_x[:, c, :], start=(c == 0), stop=(c == CHUNKS - 1)
+                )
+            q_silu = held.tile([P, EDGES], F32, name=f"q_silu{h}")
+            nc.scalar.activation(q_silu[:], q_sum[:], SILU, bias=dist_b[h])
             message = held.tile([P, EDGES], F32, name=f"message{h}")
-            nc.vector.tensor_mul(message[:], p_silu[:], q_act[h][:])
+            nc.vector.tensor_mul(message[:], p_act[h][:], q_silu[:])
             queue = nc.sync if h % 2 == 0 else nc.scalar
             queue.dma_start(out[features, :], message[:])

@@ -1,22 +1,19 @@
 import concourse.mybir as mybir
-from concourse.masks import make_identity
 
 BF16, F32, U16 = mybir.dt.bfloat16, mybir.dt.float32, mybir.dt.uint16
 SILU = mybir.ActivationFunctionType.Silu
 
 P = 128
 NODES = 2048
+GROUPS = 4
+BLOCKS = 4
 EDGES = 256
 FEATURES = 256
 HALVES = FEATURES // P
 RADIAL = 512
 CHUNKS = RADIAL // P
+LAST_PIECES = 2
 LIST_COLUMNS = EDGES // 16
-GROUP = 512
-BLOCKS = GROUP // P
-GROUPS = NODES // GROUP
-SQUARE = 32
-QUARTERS = P // SQUARE
 WARM_COLUMNS = 512
 WARM_MATMULS = 4
 
@@ -28,81 +25,82 @@ def tile_messageblock_kernel(tc, table, w_src, w_dst, b_proj, x_edge, w_dist, b_
     with (
         tc.tile_pool(name="held", bufs=1) as held,
         tc.psum_pool(name="psum", bufs=1) as psum,
-        tc.psum_pool(name="flip", bufs=3) as flip,
     ):
-        offsets = held.tile([P, 2 * LIST_COLUMNS], U16, name="offsets")
-        nc.sync.dma_start(offsets[:], offs)
-
-        identity = held.tile([P, P], BF16, name="identity")
-        make_identity(nc, identity[:])
-
-        zeros = held.tile([P, WARM_COLUMNS], BF16, name="zeros")
-        nc.vector.memset(zeros[:], 0.0)
-        warm = psum.tile([P, WARM_COLUMNS], F32, name="warm")
-        for i in range(WARM_MATMULS):
-            nc.tensor.matmul(warm[:], zeros[:, 0:P], zeros[:], start=True, stop=True)
-
-        rows = []
-        for g in range(GROUPS):
-            group_rows = held.tile([P, BLOCKS, P], BF16, name=f"rows{g}")
-            queue = nc.sync if g % 2 == 0 else nc.scalar
-            queue.dma_start(
-                group_rows[:], table[g * GROUP : (g + 1) * GROUP, :].rearrange("(b p) k -> p b k", p=P)
-            )
-            rows.append(group_rows)
-
-        src_w = held.tile([P, FEATURES], BF16, name="src_w")
-        nc.sync.dma_start(src_w[:], w_src)
-        dst_w = held.tile([P, FEATURES], BF16, name="dst_w")
-        nc.scalar.dma_start(dst_w[:], w_dst)
-
-        bias_runs = held.tile([P, P], F32, name="bias_runs", align_bytes=64)
-        nc.vector.memset(bias_runs[:], 0.0)
-        run_slots = bias_runs[:, 0 : HALVES * SQUARE].rearrange("(r s) (h i) -> s r h i", s=SQUARE, i=SQUARE)
-        nc.sync.dma_start(run_slots[0], b_dist.rearrange("(h r i) o -> r h (i o)", h=HALVES, r=QUARTERS))
-        nc.scalar.dma_start(run_slots[1], b_proj.rearrange("(h r i) o -> r h (i o)", h=HALVES, r=QUARTERS))
-        biases = held.tile([P, P], F32, name="biases", align_bytes=64)
-        nc.vector.transpose(biases[:], bias_runs[:])
-        dist_b = [biases[:, h * SQUARE : h * SQUARE + 1] for h in range(HALVES)]
-        proj_b = [biases[:, h * SQUARE + 1 : h * SQUARE + 2] for h in range(HALVES)]
+        rows = held.tile([P, GROUPS, BLOCKS, P], BF16, name="rows")
+        nc.sync.dma_start(rows[:], table.rearrange("(g p i) k -> p g i k", p=P, i=BLOCKS))
 
         edge_x = held.tile([P, CHUNKS, EDGES], BF16, name="edge_x")
         nc.sync.dma_start(edge_x[:], x_edge.rearrange("(p c) e -> p c e", c=CHUNKS))
         dist_w = held.tile([P, CHUNKS, FEATURES], BF16, name="dist_w")
-        nc.scalar.dma_start(dist_w[:], w_dist.rearrange("(p c) m -> p c m", c=CHUNKS))
+        nc.sync.dma_start(dist_w[:], w_dist.rearrange("(p c) m -> p c m", c=CHUNKS))
+
+        offsets = held.tile([P, 2 * LIST_COLUMNS], U16, name="offsets")
+        nc.sync.dma_start(offsets[:], offs)
+        src_w = held.tile([P, FEATURES], BF16, name="src_w")
+        nc.sync.dma_start(src_w[:], w_src)
+        dst_w = held.tile([P, FEATURES], BF16, name="dst_w")
+        nc.sync.dma_start(dst_w[:], w_dst)
+
+        distance = held.tile([P, P], F32, name="distance")
+        nc.gpsimd.iota(
+            distance[:], pattern=[[1, P]], base=0, channel_multiplier=-1, allow_small_or_imprecise_dtypes=True
+        )
+        identity = held.tile([P, P], BF16, name="identity")
+        nc.vector.tensor_single_scalar(identity[:], distance[:], 0.0, mybir.AluOpType.is_equal)
+
+        zeros = held.tile([P, WARM_COLUMNS], BF16, name="zeros")
+        nc.vector.memset(zeros[:], 0.0)
+        warm = psum.tile([P, WARM_COLUMNS], F32, name="warm", tag="p_sum0")
+        for i in range(WARM_MATMULS):
+            nc.tensor.matmul(warm[:], zeros[:, 0:P], zeros[:], start=True, stop=True)
+
+        bias_columns = []
+        for name, bias in (("dist", b_dist), ("proj", b_proj)):
+            column_pair = held.tile([P, HALVES], F32, name=f"{name}_b")
+            nc.gpsimd.dma_start(column_pair[:], bias.rearrange("(h p) o -> p (h o)", p=P))
+            bias_columns.append([column_pair[:, h : h + 1] for h in range(HALVES)])
+        dist_b, proj_b = bias_columns
 
         table_load = held.tile([P, 1], F32, name="table_load")
         nc.scalar.activation(table_load[:], zeros[:, 0:1], SILU)
 
         table_t = held.tile([P, NODES], BF16, name="table_t")
         for g in range(GROUPS):
-            flipped = flip.tile([P, GROUP], BF16, name="flipped")
-            for b in range(BLOCKS):
-                nc.tensor.transpose(flipped[:, b * P : (b + 1) * P], rows[g][:, b, :], identity[:])
-            nc.vector.tensor_copy(table_t[:, g * GROUP : (g + 1) * GROUP], flipped[:])
+            flipped = psum.tile([P, BLOCKS, P], BF16, name=f"flipped{g}")
+            for i in range(BLOCKS):
+                nc.tensor.transpose(flipped[:, i], rows[:, g, i], identity[:])
+            columns = table_t[:, g * BLOCKS * P : (g + 1) * BLOCKS * P].rearrange("k (p i) -> k p i", i=BLOCKS)
+            in_order = flipped[:].rearrange("k i p -> k p i")
+            if g % 2 == 0:
+                nc.vector.tensor_copy(columns, in_order)
+            else:
+                nc.scalar.copy(columns, in_order)
 
-        sources = table_t[:].indirect(offsets[:, 0:LIST_COLUMNS])
-        targets = table_t[:].indirect(offsets[:, LIST_COLUMNS : 2 * LIST_COLUMNS])
-        p_act = []
+        q_act = []
         for h in range(HALVES):
             features = slice(h * P, (h + 1) * P)
-            p_sum = psum.tile([P, EDGES], F32, name=f"p_sum{h}")
-            nc.tensor.matmul(p_sum[:], src_w[:, features], sources, start=True, stop=False)
-            nc.tensor.matmul(p_sum[:], dst_w[:, features], targets, start=False, stop=True)
-            p_silu = held.tile([P, EDGES], F32, name=f"p_silu{h}")
-            nc.scalar.activation(p_silu[:], p_sum[:], SILU, bias=proj_b[h])
-            p_act.append(p_silu)
-
-        for h in range(HALVES):
-            features = slice(h * P, (h + 1) * P)
-            q_sum = psum.tile([P, EDGES], F32, name=f"q_sum{h}")
+            q_sum = psum.tile([P, EDGES], F32, name=f"q_sum{h}", tag=f"flipped{h}")
             for c in range(CHUNKS):
                 nc.tensor.matmul(
                     q_sum[:], dist_w[:, c, features], edge_x[:, c, :], start=(c == 0), stop=(c == CHUNKS - 1)
                 )
             q_silu = held.tile([P, EDGES], F32, name=f"q_silu{h}")
             nc.scalar.activation(q_silu[:], q_sum[:], SILU, bias=dist_b[h])
+            q_act.append(q_silu)
+
+        sources = table_t[:].indirect(offsets[:, 0:LIST_COLUMNS])
+        targets = table_t[:].indirect(offsets[:, LIST_COLUMNS : 2 * LIST_COLUMNS])
+        for h in range(HALVES):
+            features = slice(h * P, (h + 1) * P)
+            p_sum = psum.tile([P, EDGES], F32, name=f"p_sum{h}")
+            nc.tensor.matmul(p_sum[:], src_w[:, features], sources, start=True, stop=False)
+            nc.tensor.matmul(p_sum[:], dst_w[:, features], targets, start=False, stop=True)
             message = held.tile([P, EDGES], F32, name=f"message{h}")
-            nc.vector.tensor_mul(message[:], p_act[h][:], q_silu[:])
-            queue = nc.sync if h % 2 == 0 else nc.scalar
-            queue.dma_start(out[features, :], message[:])
+            pieces = LAST_PIECES if h == HALVES - 1 else 1
+            width = EDGES // pieces
+            for piece in range(pieces):
+                edges = slice(piece * width, (piece + 1) * width)
+                p_silu = held.tile([P, width], F32, name=f"p_silu{h}_{piece}")
+                nc.scalar.activation(p_silu[:], p_sum[:, edges], SILU, bias=proj_b[h])
+                nc.vector.tensor_mul(message[:, edges], p_silu[:], q_act[h][:, edges])
+            nc.sync.dma_start(out[features, :], message[:])

@@ -1,4 +1,5 @@
 import concourse.mybir as mybir
+from concourse.masks import make_identity
 
 BF16, F32, U16 = mybir.dt.bfloat16, mybir.dt.float32, mybir.dt.uint16
 SILU = mybir.ActivationFunctionType.Silu
@@ -11,7 +12,7 @@ EDGES = 256
 FEATURES = 256
 HALVES = FEATURES // P
 RADIAL = 512
-CHUNKS = RADIAL // P
+CHUNKS = RADIAL // 2 // P
 LAST_PIECES = 2
 LIST_COLUMNS = EDGES // 16
 WARM_COLUMNS = 512
@@ -26,27 +27,31 @@ def tile_messageblock_kernel(tc, table, w_src, w_dst, b_proj, x_edge, w_dist, b_
         tc.tile_pool(name="held", bufs=1) as held,
         tc.psum_pool(name="psum", bufs=1) as psum,
     ):
-        rows = held.tile([P, GROUPS, BLOCKS, P], BF16, name="rows")
-        nc.sync.dma_start(rows[:], table.rearrange("(g p i) k -> p g i k", p=P, i=BLOCKS))
+        rows = []
+        for half, queue in enumerate((nc.sync, nc.scalar)):
+            half_rows = held.tile([P, GROUPS // 2, BLOCKS, P], BF16, name=f"rows{half}")
+            nodes = slice(half * NODES // 2, (half + 1) * NODES // 2)
+            queue.dma_start(half_rows[:], table[nodes, :].rearrange("(g p i) k -> p g i k", p=P, i=BLOCKS))
+            rows += [half_rows[:, g] for g in range(GROUPS // 2)]
 
-        edge_x = held.tile([P, CHUNKS, EDGES], BF16, name="edge_x")
-        nc.sync.dma_start(edge_x[:], x_edge.rearrange("(p c) e -> p c e", c=CHUNKS))
-        dist_w = held.tile([P, CHUNKS, FEATURES], BF16, name="dist_w")
-        nc.sync.dma_start(dist_w[:], w_dist.rearrange("(p c) m -> p c m", c=CHUNKS))
+        q_operands = []
+        for half in range(2):
+            radial = slice(half * RADIAL // 2, (half + 1) * RADIAL // 2)
+            edge_x = held.tile([P, CHUNKS, EDGES], BF16, name=f"edge_x{half}")
+            nc.sync.dma_start(edge_x[:], x_edge[radial, :].rearrange("(p c) e -> p c e", c=CHUNKS))
+            dist_w = held.tile([P, CHUNKS, FEATURES], BF16, name=f"dist_w{half}")
+            nc.scalar.dma_start(dist_w[:], w_dist[radial, :].rearrange("(p c) m -> p c m", c=CHUNKS))
+            q_operands.append((edge_x, dist_w))
 
         offsets = held.tile([P, 2 * LIST_COLUMNS], U16, name="offsets")
         nc.sync.dma_start(offsets[:], offs)
         src_w = held.tile([P, FEATURES], BF16, name="src_w")
         nc.sync.dma_start(src_w[:], w_src)
         dst_w = held.tile([P, FEATURES], BF16, name="dst_w")
-        nc.sync.dma_start(dst_w[:], w_dst)
+        nc.scalar.dma_start(dst_w[:], w_dst)
 
-        distance = held.tile([P, P], F32, name="distance")
-        nc.gpsimd.iota(
-            distance[:], pattern=[[1, P]], base=0, channel_multiplier=-1, allow_small_or_imprecise_dtypes=True
-        )
         identity = held.tile([P, P], BF16, name="identity")
-        nc.vector.tensor_single_scalar(identity[:], distance[:], 0.0, mybir.AluOpType.is_equal)
+        make_identity(nc, identity[:])
 
         zeros = held.tile([P, WARM_COLUMNS], BF16, name="zeros")
         nc.vector.memset(zeros[:], 0.0)
@@ -57,7 +62,7 @@ def tile_messageblock_kernel(tc, table, w_src, w_dst, b_proj, x_edge, w_dist, b_
         bias_columns = []
         for name, bias in (("dist", b_dist), ("proj", b_proj)):
             column_pair = held.tile([P, HALVES], F32, name=f"{name}_b")
-            nc.gpsimd.dma_start(column_pair[:], bias.rearrange("(h p) o -> p (h o)", p=P))
+            nc.sync.dma_start(column_pair[:], bias.rearrange("(h p) o -> p (h o)", p=P))
             bias_columns.append([column_pair[:, h : h + 1] for h in range(HALVES)])
         dist_b, proj_b = bias_columns
 
@@ -68,7 +73,7 @@ def tile_messageblock_kernel(tc, table, w_src, w_dst, b_proj, x_edge, w_dist, b_
         for g in range(GROUPS):
             flipped = psum.tile([P, BLOCKS, P], BF16, name=f"flipped{g}")
             for i in range(BLOCKS):
-                nc.tensor.transpose(flipped[:, i], rows[:, g, i], identity[:])
+                nc.tensor.transpose(flipped[:, i], rows[g][:, i], identity[:])
             columns = table_t[:, g * BLOCKS * P : (g + 1) * BLOCKS * P].rearrange("k (p i) -> k p i", i=BLOCKS)
             in_order = flipped[:].rearrange("k i p -> k p i")
             if g % 2 == 0:
@@ -76,14 +81,19 @@ def tile_messageblock_kernel(tc, table, w_src, w_dst, b_proj, x_edge, w_dist, b_
             else:
                 nc.scalar.copy(columns, in_order)
 
+        q_sums = [psum.tile([P, EDGES], F32, name=f"q_sum{h}", tag=f"flipped{h}") for h in range(HALVES)]
+        for half, (edge_x, dist_w) in enumerate(q_operands):
+            for h, q_sum in enumerate(q_sums):
+                for c in range(CHUNKS):
+                    nc.tensor.matmul(
+                        q_sum[:],
+                        dist_w[:, c, h * P : (h + 1) * P],
+                        edge_x[:, c, :],
+                        start=(half == 0 and c == 0),
+                        stop=(half == 1 and c == CHUNKS - 1),
+                    )
         q_act = []
-        for h in range(HALVES):
-            features = slice(h * P, (h + 1) * P)
-            q_sum = psum.tile([P, EDGES], F32, name=f"q_sum{h}", tag=f"flipped{h}")
-            for c in range(CHUNKS):
-                nc.tensor.matmul(
-                    q_sum[:], dist_w[:, c, features], edge_x[:, c, :], start=(c == 0), stop=(c == CHUNKS - 1)
-                )
+        for h, q_sum in enumerate(q_sums):
             q_silu = held.tile([P, EDGES], F32, name=f"q_silu{h}")
             nc.scalar.activation(q_silu[:], q_sum[:], SILU, bias=dist_b[h])
             q_act.append(q_silu)

import concourse.mybir as mybir
from concourse.masks import make_identity

BF16, F32, U16 = mybir.dt.bfloat16, mybir.dt.float32, mybir.dt.uint16
SILU = mybir.ActivationFunctionType.Silu

P = 128
NODES = 2048
GROUPS = 4
BLOCKS = 4
EDGES = 256
FEATURES = 256
HALVES = FEATURES // P
RADIAL = 512
CHUNKS = RADIAL // 2 // P
LAST_PIECES = 2
LIST_COLUMNS = EDGES // 16
WARM_COLUMNS = 512
WARM_MATMULS = 4

FLOPS = 2 * FEATURES * EDGES * (P + P + RADIAL)


def tile_messageblock_kernel(tc, table, w_src, w_dst, b_proj, x_edge, w_dist, b_dist, offs, out):
    nc = tc.nc
    with (
        tc.tile_pool(name="held", bufs=1) as held,
        tc.psum_pool(name="psum", bufs=1) as psum,
    ):
        rows = []
        for half, queue in enumerate((nc.sync, nc.scalar)):
            half_rows = held.tile([P, GROUPS // 2, BLOCKS, P], BF16, name=f"rows{half}")
            nodes = slice(half * NODES // 2, (half + 1) * NODES // 2)
            queue.dma_start(half_rows[:], table[nodes, :].rearrange("(g p i) k -> p g i k", p=P, i=BLOCKS))
            rows += [half_rows[:, g] for g in range(GROUPS // 2)]

        q_operands = []
        for half in range(2):
            radial = slice(half * RADIAL // 2, (half + 1) * RADIAL // 2)
            edge_x = held.tile([P, CHUNKS, EDGES], BF16, name=f"edge_x{half}")
            nc.sync.dma_start(edge_x[:], x_edge[radial, :].rearrange("(p c) e -> p c e", c=CHUNKS))
            dist_w = held.tile([P, CHUNKS, FEATURES], BF16, name=f"dist_w{half}")
            nc.scalar.dma_start(dist_w[:], w_dist[radial, :].rearrange("(p c) m -> p c m", c=CHUNKS))
            q_operands.append((edge_x, dist_w))

        offsets = held.tile([P, 2 * LIST_COLUMNS], U16, name="offsets")
        nc.sync.dma_start(offsets[:], offs)
        src_w = held.tile([P, FEATURES], BF16, name="src_w")
        nc.sync.dma_start(src_w[:], w_src)
        dst_w = held.tile([P, FEATURES], BF16, name="dst_w")
        nc.scalar.dma_start(dst_w[:], w_dst)

        identity = held.tile([P, P], BF16, name="identity")
        make_identity(nc, identity[:])

        zeros = held.tile([P, WARM_COLUMNS], BF16, name="zeros")
        nc.vector.memset(zeros[:], 0.0)
        warm = psum.tile([P, WARM_COLUMNS], F32, name="warm", tag="p_sum0")
        for i in range(WARM_MATMULS):
            nc.tensor.matmul(warm[:], zeros[:, 0:P], zeros[:], start=True, stop=True)

        bias_columns = []
        for name, bias in (("dist", b_dist), ("proj", b_proj)):
            column_pair = held.tile([P, HALVES], F32, name=f"{name}_b")
            nc.sync.dma_start(column_pair[:], bias.rearrange("(h p) o -> p (h o)", p=P))
            bias_columns.append([column_pair[:, h : h + 1] for h in range(HALVES)])
        dist_b, proj_b = bias_columns

        table_load = held.tile([P, 1], F32, name="table_load")
        nc.scalar.activation(table_load[:], zeros[:, 0:1], SILU)

        table_t = held.tile([P, NODES], BF16, name="table_t")
        for g in range(GROUPS):
            flipped = psum.tile([P, BLOCKS, P], BF16, name=f"flipped{g}")
            for i in range(BLOCKS):
                nc.tensor.transpose(flipped[:, i], rows[g][:, i], identity[:])
            columns = table_t[:, g * BLOCKS * P : (g + 1) * BLOCKS * P].rearrange("k (p i) -> k p i", i=BLOCKS)
            in_order = flipped[:].rearrange("k i p -> k p i")
            if g % 2 == 0:
                nc.vector.tensor_copy(columns, in_order)
            else:
                nc.scalar.copy(columns, in_order)

        q_sums = [psum.tile([P, EDGES], F32, name=f"q_sum{h}", tag=f"flipped{h}") for h in range(HALVES)]
        for half, (edge_x, dist_w) in enumerate(q_operands):
            for h, q_sum in enumerate(q_sums):
                for c in range(CHUNKS):
                    nc.tensor.matmul(
                        q_sum[:],
                        dist_w[:, c, h * P : (h + 1) * P],
                        edge_x[:, c, :],
                        start=(half == 0 and c == 0),
                        stop=(half == 1 and c == CHUNKS - 1),
                    )
        q_act = []
        for h, q_sum in enumerate(q_sums):
            q_silu = held.tile([P, EDGES], F32, name=f"q_silu{h}")
            nc.scalar.activation(q_silu[:], q_sum[:], SILU, bias=dist_b[h])
            q_act.append(q_silu)

        sources = table_t[:].indirect(offsets[:, 0:LIST_COLUMNS])
        targets = table_t[:].indirect(offsets[:, LIST_COLUMNS : 2 * LIST_COLUMNS])
        for h in range(HALVES):
            features = slice(h * P, (h + 1) * P)
            p_sum = psum.tile([P, EDGES], F32, name=f"p_sum{h}")
            nc.tensor.matmul(p_sum[:], src_w[:, features], sources, start=True, stop=False)
            nc.tensor.matmul(p_sum[:], dst_w[:, features], targets, start=False, stop=True)
            message = held.tile([P, EDGES], F32, name=f"message{h}")
            pieces = LAST_PIECES if h == HALVES - 1 else 1
            width = EDGES // pieces
            for piece in range(pieces):
                edges = slice(piece * width, (piece + 1) * width)
                p_silu = held.tile([P, width], F32, name=f"p_silu{h}_{piece}")
                nc.scalar.activation(p_silu[:], p_sum[:, edges], SILU, bias=proj_b[h])
                nc.vector.tensor_mul(message[:, edges], p_silu[:], q_act[h][:, edges])
            nc.sync.dma_start(out[features, :], message[:])
